import numpy as np
import ml_dtypes


def mxq(x, axis, fmt="e4m3"):
    dtype, down = {"e4m3": (ml_dtypes.float8_e4m3fn, 7), "e5m2": (ml_dtypes.float8_e5m2, 14)}[fmt]
    v = np.moveaxis(np.asarray(x, np.float32).astype(ml_dtypes.bfloat16).astype(np.float64), axis, -1)
    blocks = v.reshape(v.shape[:-1] + (-1, 32))
    amax = np.abs(blocks).max(-1, keepdims=True)
    byte = np.maximum(np.where(amax > 0, np.frexp(amax)[1] - 1 + 127, 0) - down, 1)
    scale = np.exp2(byte - 127.0)
    codes = (blocks / scale).astype(np.float32).astype(dtype).astype(np.float64)
    return np.moveaxis((codes * scale).reshape(v.shape), -1, axis)


WIDE = False


def mx_kscale(k):
    if not WIDE:
        return np.ones(k)
    levels = np.array([10, -10, 5, -5, 0])
    if k % 512:
        return np.exp2(np.random.permutation(np.resize(levels, k // 32))).repeat(32)
    a = np.empty((k // 512, 16))
    for p in range(k // 512):
        a[p, :8] = np.random.permutation(np.resize(levels, 8))
        for g in range(8):
            far = levels[np.abs(levels - a[p, g]) >= 10]
            a[p, g + 8] = far[np.random.randint(len(far))]
    return np.exp2(a.ravel()).repeat(32)


BF16 = ml_dtypes.bfloat16


def bf(x):
    return np.asarray(x, np.float32).astype(BF16)


def f64(x):
    return np.asarray(x).astype(np.float64)


B, K, NH, N = 512, 2048, 4096, 1024
EPSILON = 0.1


def setup_inputs():
    s = mx_kscale(K)
    g = 1.0 / np.mean(1.0 / s)
    return {"x": bf(np.random.standard_normal((B, K)) * s),
            "y": bf(np.random.standard_normal((B, N)) * 12.0 / np.sqrt(K) * g),
            "beta": bf(np.random.random((K, N)) * 1.7 / np.sqrt(K) / s[:, None]),
            "bias_lin": bf(np.random.standard_normal(N) * 0.1),
            "W1": bf(-np.random.random((NH, K)) * 1.7 / np.sqrt(K) / s[None, :]),
            "W2": bf(np.random.random((N, NH)) * (0.5 + np.random.random((N, 1))) * 2.0 / NH**2),
            "bias1": bf(np.random.standard_normal(NH) * 0.1),
            "bias2": bf(np.random.standard_normal(N) * 0.1),
            "adv": 1}


def core(x, y, beta, bias_lin, W1, W2, bias1, bias2, adv):
    xq = mxq(f64(x), 1, "e4m3")
    lin = (xq @ mxq(f64(beta), 0, "e4m3")) + f64(bias_lin)
    if adv:
        beta_norm = np.sum(np.abs(f64(beta)), axis=0)
        lin = lin - EPSILON * f64(y) * beta_norm
    if adv:
        one = NH * np.sum(f64(W2), axis=1) + f64(bias2)
        one = np.broadcast_to(one, lin.shape)
    else:
        h = np.maximum((xq @ mxq(f64(W1), 1, "e4m3").T) + f64(bias1), 0.0)
        one = (mxq(h, 1, "e4m3") @ mxq(f64(W2), 1, "e4m3").T) + f64(bias2)
    return lin + one


def e4m3fn_bytes(y):
    return np.clip(np.asarray(y, np.float64), -448.0, 448.0).astype(np.float32).astype(ml_dtypes.float8_e4m3fn).view(np.uint8)


def reference(x, y, beta, bias_lin, W1, W2, bias1, bias2, adv):
    out = core(x, y, beta, bias_lin, W1, W2, bias1, bias2, adv)
    s = np.max(np.abs(out), axis=-1, keepdims=True) / 448.0
    return out, e4m3fn_bytes(out / s)

@@ -1,0 +1,359 @@
+from contextlib import ExitStack
+
+import concourse.mybir as mybir
+from concourse.masks import make_identity
+
+F32 = mybir.dt.float32
+BF16 = mybir.dt.bfloat16
+I32 = mybir.dt.int32
+U32 = mybir.dt.uint32
+U8 = mybir.dt.uint8
+FP8X4 = mybir.dt.float8_e4m3fn_x4
+FP8 = mybir.dt.float8_e4m3fn
+ALU = mybir.AluOpType
+ACT = mybir.ActivationFunctionType
+AX = mybir.AxisListType
+
+B, K, NH, N = 512, 2048, 4096, 1024
+P = 128
+BT = B // P
+G = K // 512
+JT = N // P
+HALF = 512
+
+FLOPS = 2 * B * K * N
+BYTES = 2 * (B * K + B * N + K * N + N * NH + 2 * N) + 5 * B * N
+
+CV = 512
+PARTS0 = ((0, 256, "v"), (256, 512, "s"), (512, 768, "v"), (768, 1024, "s"))
+PARTS = ((0, CV, "v"), (CV, N, "s"))
+PLAN = ((0, NH, 0), (NH, 0, 0), (0, NH, 0), (NH, 0, 0),
+        (0, 0, NH), (0, NH // 2, NH // 2), (0, NH, 0), (1536, NH - 1536, 0))
+BLOCKS = ((0, 4, "g"), (4, 4, "v"))
+
+
+def tile_advresnet_kernel(tc, x, y, beta, bias_lin, W1, W2, bias1, bias2, adv, out_0, out_1):
+    nc = tc.nc
+    assert adv == 1
+    with ExitStack() as ctx:
+        const = ctx.enter_context(tc.tile_pool(name="const", bufs=1))
+        keep = ctx.enter_context(tc.tile_pool(name="keep", bufs=1))
+        work = ctx.enter_context(tc.tile_pool(name="work", bufs=2))
+        psum = ctx.enter_context(tc.psum_pool(name="psum", bufs=2))
+
+        raw = []
+        for g in range(G):
+            rows = beta[512 * g:512 * (g + 1), :].rearrange("(p t) c -> p t c", t=4)
+            chunks = []
+            cuts = PARTS0 if g == 0 else ((0, N, "-"),)
+            for ci in range(len(cuts)):
+                c0, c1, who = cuts[ci]
+                r = keep.tile([P, 4, c1 - c0], BF16, name="raw%d_%d" % (g, ci), tag="raw%d_%d" % (g, ci))
+                nc.sync.dma_start(out=r[:], in_=rows[:, :, c0:c1])
+                chunks.append((c0, c1, r))
+            raw.append(chunks)
+        y_sb = keep.tile([P, BT, N], BF16, name="y_sb", tag="y_sb")
+        nc.sync.dma_start(out=y_sb[:], in_=y.rearrange("(t p) c -> p t c", p=P))
+        x_sb = []
+        for bt in range(BT):
+            xl = keep.tile([P, K], BF16, name="x_sb%d" % bt, tag="x_sb%d" % bt)
+            nc.sync.dma_start(out=xl[:], in_=x[P * bt:P * (bt + 1), :])
+            x_sb.append(xl)
+        w2 = []
+        for t in range(JT):
+            rows = W2[P * t:P * (t + 1), :]
+            tiles = []
+            c0 = 0
+            for k in range(3):
+                n = PLAN[t][k]
+                wt = None
+                if n > 0:
+                    wt = keep.tile([P, n], BF16, name="w2_%d_%d" % (t, k), tag="w2_%d_%d" % (t, k))
+                    nc.sync.dma_start(out=wt[:], in_=rows[:, c0:c0 + n])
+                tiles.append(wt)
+                c0 += n
+            w2.append(tiles)
+
+        zeros = const.tile([P, 1], F32, name="zeros", tag="zeros")
+        nc.vector.memset(zeros[:], 0.0)
+        warm = const.tile([P, 1], F32, name="warm", tag="warm")
+        nc.scalar.activation(out=warm[:], in_=zeros[:], func=ACT.Copy)
+        two_b = const.tile([P, 1], BF16, name="two_b", tag="two_b")
+        nc.vector.memset(two_b[:], 2.0)
+        neg_b = const.tile([P, 1], BF16, name="neg_b", tag="neg_b")
+        nc.vector.memset(neg_b[:], -1.0)
+        brow = const.tile([P, P], BF16, name="brow", tag="brow")
+        nc.vector.memset(brow[:], 0.0)
+        nc.scalar.dma_start(out=brow[0:JT, :], in_=bias_lin.rearrange("(c p) -> c p", p=P))
+        nc.scalar.dma_start(out=brow[JT:2 * JT, :], in_=bias2.rearrange("(c p) -> c p", p=P))
+        ident_f = const.tile([P, P], F32, name="ident_f", tag="ident_f")
+        make_identity(nc, ident_f[:])
+        ident_b = const.tile([P, P], BF16, name="ident_b", tag="ident_b")
+        make_identity(nc, ident_b[:])
+        sel = const.tile([P, JT], BF16, name="sel", tag="sel")
+        nc.vector.tensor_tensor(out=sel[:], in0=ident_f[:, 0:JT], in1=ident_f[:, JT:2 * JT], op=ALU.add)
+
+        small = psum.tile([P, 32 * JT + JT], F32, name="small", tag="small", bufs=1)
+        bc = keep.tile([P, G, N], U32, name="bc", tag="bc", align_bytes=64)
+        bs = keep.tile([P, G, N], U8, name="bs", tag="bs", align_bytes=64)
+        xc = []
+        xs = []
+        for bt in range(BT):
+            xct = keep.tile([P, G * P], U32, name="xc%d" % bt, tag="xc%d" % bt, align_bytes=64)
+            xst = keep.tile([P, G * P], U8, name="xs%d" % bt, tag="xs%d" % bt, align_bytes=64)
+            xc.append(xct)
+            xs.append(xst)
+        o = keep.tile([P, BT, N], F32, name="o", tag="o")
+        o8 = keep.tile([P, BT, N], FP8, name="o8", tag="o8")
+        bnb = keep.tile([P, N], F32, name="bnb", tag="bnb")
+        cbb = keep.tile([P, HALF], F32, name="cbb", tag="cbb")
+        bnv = const.tile([P, JT], F32, name="bnv", tag="bnv")
+        cb = const.tile([P, JT], F32, name="cb", tag="cb")
+        sv = const.tile([P, JT], F32, name="sv", tag="sv")
+        ss = const.tile([P, JT], F32, name="ss", tag="ss")
+        nc.vector.memset(ss[:], 0.0)
+        cv = const.tile([P, JT], F32, name="cv", tag="cv")
+        pm = const.tile([P, BT, len(BLOCKS)], F32, name="pm", tag="pm")
+        am = const.tile([P, BT], F32, name="am", tag="am")
+        rs = const.tile([P, BT], F32, name="rs", tag="rs")
+        r0 = const.tile([P, BT], F32, name="r0", tag="r0")
+        r1 = const.tile([P, BT], F32, name="r1", tag="r1")
+        junk = const.tile([P, HALF], BF16, name="junk", tag="junk")
+
+        abt = {}
+        grps = {}
+        xgs = {}
+        accs = {}
+        sps = {}
+
+        def beta_abs(g, ci):
+            if ci == 0:
+                ab = work.tile([P, 4, N], BF16, name="ab", tag="ab", bufs=2)
+                abt[g] = ab
+            c0, c1, r = raw[g][ci]
+            nc.vector.tensor_scalar(out=abt[g][:, :, c0:c1], in0=r[:], scalar1=0.0, scalar2=None, op0=ALU.max)
+
+        def beta_norm_part(g):
+            for t in range(4):
+                for jt in range(JT):
+                    col = (g * 4 + t) * JT + jt
+                    for l0, l1, r in raw[g]:
+                        if l0 <= P * jt and P * (jt + 1) <= l1:
+                            nc.tensor.matmul(out=small[:, col:col + 1], lhsT=r[:, t, P * jt - l0:P * (jt + 1) - l0],
+                                             rhs=neg_b[:, 0:1], start=True, stop=True)
+            for t in range(4):
+                for jt in range(JT):
+                    col = (16 + g * 4 + t) * JT + jt
+                    nc.tensor.matmul(out=small[:, col:col + 1], lhsT=abt[g][:, t, P * jt:P * (jt + 1)],
+                                     rhs=two_b[:, 0:1], start=True, stop=True)
+
+        def beta_copy(g, pi):
+            if g not in grps:
+                grp = work.tile([P, N, 4], BF16, name="grp", tag="grp", bufs=3, align_bytes=64)
+                grps[g] = grp
+            c0, c1, who = (PARTS0 if g == 0 else PARTS)[pi]
+            for l0, l1, r in raw[g]:
+                if l0 <= c0 and c1 <= l1:
+                    src = r[:, :, c0 - l0:c1 - l0].rearrange("p t (c i) -> p c t i", i=4)
+                    dst = grps[g][:, c0:c1, :].rearrange("p (c i) t -> p c t i", i=4)
+                    if who == "v":
+                        nc.vector.tensor_copy(out=dst, in_=src)
+                    else:
+                        nc.scalar.copy(out=dst, in_=src)
+
+        def beta_quant(g):
+            nc.vector.quantize_mx(out=bc[:, g, :].bitcast(FP8X4), scales=bs[:, g, :],
+                                  in_=grps[g][:].rearrange("p c t -> p (c t)"))
+
+        def x_turn(bt):
+            xw = x_sb[bt][:].bitcast(F32)
+            xg = work.tile([P, G, P, 4], BF16, name="xg", tag="xg", bufs=3, align_bytes=64)
+            xgs[bt] = xg
+            for gp in range(G // 2):
+                xt = psum.tile([P, 2, 2, P], F32, name="xt", tag="xt", bufs=2)
+                for g2 in range(2):
+                    g = 2 * gp + g2
+                    for u in range(2):
+                        nc.tensor.transpose(out=xt[:, g2, u, :], in_=xw[:, 256 * g + u:256 * (g + 1):2],
+                                            identity=ident_f[:])
+                nc.scalar.copy(out=xg[:, 2 * gp:2 * gp + 2, :, :].bitcast(F32),
+                               in_=xt[:].rearrange("p g u b -> p g b u"))
+
+        def x_quant(bt):
+            nc.vector.quantize_mx(out=xc[bt][:].bitcast(FP8X4), scales=xs[bt][:],
+                                  in_=xgs[bt][:].rearrange("p g b t -> p (g b t)"))
+
+        def norm_reduce():
+            nc.vector.tensor_reduce(out=bnv[:], in_=small[:, 0:32 * JT].rearrange("p (s j) -> p j s", j=JT),
+                                    axis=AX.X, op=ALU.add)
+
+        def norm_spread(h):
+            sp = psum.tile([P, HALF], F32, name="acc", tag="acc", bufs=5)
+            for q in range(4):
+                jt = 4 * h + q
+                nc.tensor.transpose(out=sp[:, P * q:P * (q + 1)], in_=bnv[:, jt:jt + 1].to_broadcast([P, P]),
+                                    identity=ident_f[:])
+            nc.scalar.activation(out=bnb[:, HALF * h:HALF * (h + 1)], in_=sp[:], func=ACT.Copy, scale=-0.1)
+
+        def y_term(bt):
+            nc.gpsimd.tensor_tensor(out=o[:, bt, :], in0=y_sb[:, bt, :], in1=bnb[:], op=ALU.mult)
+
+        def product(bt, h):
+            hs = slice(HALF * h, HALF * (h + 1))
+            acc = psum.tile([P, HALF], F32, name="acc", tag="acc", bufs=5)
+            accs[(bt, h)] = acc
+            for g in range(G):
+                gs = slice(P * g, P * (g + 1))
+                nc.tensor.matmul_mx(out=acc[:], lhsT=xc[bt][:, gs].bitcast(FP8X4), lhsT_scale=xs[bt][:, gs],
+                                    rhs=bc[:, g, hs].bitcast(FP8X4), rhs_scale=bs[:, g, hs],
+                                    start=(g == 0), stop=(g == G - 1))
+
+        def add_y_term(bt, h):
+            hs = slice(HALF * h, HALF * (h + 1))
+            nc.vector.tensor_tensor(out=o[:, bt, hs], in0=accs[(bt, h)][:], in1=o[:, bt, hs], op=ALU.add)
+
+        def w2_scalar(t):
+            ws = w2[t][0]
+            nc.scalar.activation(out=ws[:], in_=ws[:], func=ACT.Copy, scale=4096.0, accum_out=ss[:, t:t + 1])
+
+        def w2_vector(t):
+            wv = w2[t][1]
+            nc.vector.tensor_scalar(out=wv[:], in0=wv[:], scalar1=4096.0, scalar2=cb[:, t:t + 1],
+                                    op0=ALU.mult, op1=ALU.add, accum_out=sv[:, t:t + 1])
+
+        def w2_tensor(t):
+            wp = w2[t][2]
+            wacc = psum.tile([P, HALF], F32, name="xt", tag="xt", bufs=2)
+            nch = PLAN[t][2] // HALF
+            for c in range(nch):
+                nc.tensor.matmul(out=wacc[:], lhsT=ident_b[:], rhs=wp[:, HALF * c:HALF * (c + 1)],
+                                 start=(c == 0), stop=(c == nch - 1))
+            nc.scalar.activation(out=junk[:], in_=wacc[:], func=ACT.Copy, scale=4096.0, accum_out=ss[:, t:t + 1])
+
+        def const_spread(bi):
+            t0, nt, who = BLOCKS[bi]
+            nc.vector.tensor_tensor(out=cv[:, t0:t0 + nt], in0=sv[:, t0:t0 + nt], in1=ss[:, t0:t0 + nt], op=ALU.add)
+            sp = psum.tile([P, HALF], F32, name="xt", tag="xt", bufs=2)
+            sps[bi] = sp
+            for q in range(nt):
+                nc.tensor.transpose(out=sp[:, P * q:P * (q + 1)], in_=cv[:, t0 + q:t0 + q + 1].to_broadcast([P, P]),
+                                    identity=ident_f[:])
+
+        def block_cols(bi):
+            t0, nt, who = BLOCKS[bi]
+            return slice(P * t0, P * (t0 + nt)), nt * P
+
+        def const_add_gpsimd_prepare(bi):
+            js, w = block_cols(bi)
+            nc.scalar.copy(out=cbb[:, 0:w], in_=sps[bi][:, 0:w])
+
+        def const_add_gpsimd(bi, bt):
+            js, w = block_cols(bi)
+            nc.gpsimd.tensor_tensor(out=o[:, bt, js], in0=o[:, bt, js], in1=cbb[:, 0:w], op=ALU.add)
+            nc.sync.dma_start(out=out_0[P * bt:P * (bt + 1), js], in_=o[:, bt, js])
+
+        def const_add_vector(bi):
+            js, w = block_cols(bi)
+            nc.vector.tensor_tensor(out=o[:, :, js], in0=o[:, :, js],
+                                    in1=sps[bi][:, 0:w].unsqueeze(1).to_broadcast([P, BT, w]), op=ALU.add)
+            nc.sync.dma_start(out=out_0.rearrange("(t p) c -> p t c", p=P)[:, :, js], in_=o[:, :, js])
+
+        def row_max(bi, bt):
+            js, w = block_cols(bi)
+            nc.vector.tensor_reduce(out=pm[:, bt, bi:bi + 1], in_=o[:, bt, js], axis=AX.X, op=ALU.max,
+                                    apply_absolute_value=True)
+
+        with tc.manual_schedule():
+            beta_abs(0, 0)
+            beta_copy(0, 0)
+            beta_copy(0, 1)
+            beta_abs(0, 1)
+            beta_abs(0, 2)
+            beta_copy(0, 2)
+            beta_copy(0, 3)
+            beta_abs(0, 3)
+            beta_norm_part(0)
+            beta_quant(0)
+            beta_abs(1, 0)
+            beta_norm_part(1)
+            beta_copy(1, 0)
+            beta_copy(1, 1)
+            beta_abs(2, 0)
+            beta_norm_part(2)
+            beta_abs(3, 0)
+            beta_norm_part(3)
+            beta_quant(1)
+            beta_copy(2, 0)
+            beta_copy(2, 1)
+            nc.tensor.matmul(out=small[:, 32 * JT:33 * JT], lhsT=brow[:], rhs=sel[:], start=True, stop=True)
+            nc.vector.tensor_copy(out=cb[:], in_=small[:, 32 * JT:33 * JT])
+            nc.vector.tensor_copy(out=sv[:], in_=small[:, 32 * JT:33 * JT])
+            norm_reduce()
+            beta_copy(3, 1)
+            x_turn(0)
+            norm_spread(0)
+            norm_spread(1)
+            beta_quant(2)
+            beta_copy(3, 0)
+            for bt in range(BT):
+                y_term(bt)
+            x_turn(1)
+            x_turn(2)
+            x_quant(0)
+            beta_quant(3)
+            x_turn(3)
+            x_quant(1)
+            product(0, 0)
+            product(0, 1)
+            w2_vector(0)
+            x_quant(2)
+            x_quant(3)
+            w2_scalar(1)
+            add_y_term(0, 0)
+            add_y_term(0, 1)
+            product(1, 0)
+            product(1, 1)
+            w2_vector(2)
+            w2_scalar(3)
+            add_y_term(1, 0)
+            add_y_term(1, 1)
+            product(2, 0)
+            product(2, 1)
+            add_y_term(2, 0)
+            add_y_term(2, 1)
+            product(3, 0)
+            product(3, 1)
+            add_y_term(3, 0)
+            add_y_term(3, 1)
+            w2_tensor(4)
+            const_spread(0)
+            const_add_gpsimd_prepare(0)
+            w2_tensor(5)
+            for bt in range(BT):
+                const_add_gpsimd(0, bt)
+            w2_vector(5)
+            w2_vector(6)
+            w2_scalar(7)
+            w2_vector(7)
+            row_max(0, 0)
+            const_spread(1)
+            row_max(0, 1)
+            const_add_vector(1)
+            row_max(0, 2)
+            row_max(1, 0)
+            row_max(1, 1)
+            row_max(0, 3)
+            nc.vector.reciprocal(out=r0[:], in_=pm[:, :, 0])
+            row_max(1, 2)
+            row_max(1, 3)
+            nc.vector.tensor_scalar(out=r0[:], in0=r0[:], scalar1=448.0, scalar2=None, op0=ALU.mult)
+            nc.vector.reciprocal(out=r1[:], in_=pm[:, :, 1])
+            nc.vector.scalar_tensor_tensor(out=rs[:], in0=r1[:], scalar=448.0, in1=r0[:], op0=ALU.mult, op1=ALU.min)
+            for bt in (3, 0, 1, 2):
+                if bt == 3:
+                    nc.scalar.activation(out=o8[:, bt, :], in_=o[:, bt, :], func=ACT.Identity, scale=rs[:, bt:bt + 1],
+                                         bias=zeros[:, 0:1], saturate=False)
+                else:
+                    nc.vector.tensor_scalar(out=o8[:, bt, :], in0=o[:, bt, :], scalar1=rs[:, bt:bt + 1], scalar2=None,
+                                            op0=ALU.mult, saturate=False)
+                nc.sync.dma_start(out=out_1[P * bt:P * (bt + 1), :], in_=o8[:, bt, :].bitcast(U8))

@@ -27,9 +27,12 @@ BYTES = 2 * (B * K + B * N + K * N + N * NH + 2 * N) + 5 * B * N
 CV = 512
 PARTS0 = ((0, 256, "v"), (256, 512, "s"), (512, 768, "v"), (768, 1024, "s"))
 PARTS = ((0, CV, "v"), (CV, N, "s"))
-PLAN = ((0, NH, 0), (NH, 0, 0), (0, NH, 0), (NH, 0, 0),
-        (0, 0, NH), (0, NH // 2, NH // 2), (0, NH, 0), (1536, NH - 1536, 0))
-BLOCKS = ((0, 4, "g"), (4, 4, "v"))
+PLAN = ((0, NH), (NH, 0), (0, NH), (NH, 0))
+NT = len(PLAN)
+BLOCKS = ((0, 4), (4, 2), (6, 1), (7, 1))
+RB = 32
+QW = NH // 4
+NCH = (JT - NT) * P // RB
 
 
 def tile_advresnet_kernel(tc, x, y, beta, bias_lin, W1, W2, bias1, bias2, adv, out_0, out_1):
@@ -60,11 +63,11 @@ def tile_advresnet_kernel(tc, x, y, beta, bias_lin, W1, W2, bias1, bias2, adv, o
             nc.sync.dma_start(out=xl[:], in_=x[P * bt:P * (bt + 1), :])
             x_sb.append(xl)
         w2 = []
-        for t in range(JT):
+        for t in range(NT):
             rows = W2[P * t:P * (t + 1), :]
             tiles = []
             c0 = 0
-            for k in range(3):
+            for k in range(2):
                 n = PLAN[t][k]
                 wt = None
                 if n > 0:
@@ -73,27 +76,42 @@ def tile_advresnet_kernel(tc, x, y, beta, bias_lin, W1, W2, bias1, bias2, adv, o
                 tiles.append(wt)
                 c0 += n
             w2.append(tiles)
+        quarters = W2.rearrange("j (h q) -> (j h) q", q=QW)
+        wq = []
+        for d in range(NCH // 4 - 1):
+            wt = keep.tile([P, 4, QW], BF16, name="wq%d" % d, tag="wq%d" % d)
+            first = 4 * P * NT + 4 * P * d
+            nc.sync.dma_start(out=wt[:], in_=quarters[first:first + 4 * P, :].rearrange("(c p) q -> p c q", p=P))
+            for c in range(4):
+                wq.append(wt[:, c, :])
+        for c in range(NCH - 4, NCH):
+            wt = keep.tile([P, QW], BF16, name="wql%d" % c, tag="wql%d" % c)
+            first = 4 * P * NT + P * c
+            nc.sync.dma_start(out=wt[:], in_=quarters[first:first + P, :])
+            wq.append(wt[:])
 
         zeros = const.tile([P, 1], F32, name="zeros", tag="zeros")
         nc.vector.memset(zeros[:], 0.0)
         warm = const.tile([P, 1], F32, name="warm", tag="warm")
         nc.scalar.activation(out=warm[:], in_=zeros[:], func=ACT.Copy)
-        two_b = const.tile([P, 1], BF16, name="two_b", tag="two_b")
-        nc.vector.memset(two_b[:], 2.0)
-        neg_b = const.tile([P, 1], BF16, name="neg_b", tag="neg_b")
-        nc.vector.memset(neg_b[:], -1.0)
+        one_b = const.tile([P, 1], BF16, name="one_b", tag="one_b")
+        nc.vector.memset(one_b[:], 1.0)
+        ones_f = const.tile([P, P], F32, name="ones_f", tag="ones_f")
+        nc.vector.memset(ones_f[:], 1.0)
         brow = const.tile([P, P], BF16, name="brow", tag="brow")
         nc.vector.memset(brow[:], 0.0)
         nc.scalar.dma_start(out=brow[0:JT, :], in_=bias_lin.rearrange("(c p) -> c p", p=P))
         nc.scalar.dma_start(out=brow[JT:2 * JT, :], in_=bias2.rearrange("(c p) -> c p", p=P))
         ident_f = const.tile([P, P], F32, name="ident_f", tag="ident_f")
         make_identity(nc, ident_f[:])
-        ident_b = const.tile([P, P], BF16, name="ident_b", tag="ident_b")
-        make_identity(nc, ident_b[:])
         sel = const.tile([P, JT], BF16, name="sel", tag="sel")
         nc.vector.tensor_tensor(out=sel[:], in0=ident_f[:, 0:JT], in1=ident_f[:, JT:2 * JT], op=ALU.add)
+        sel32f = const.tile([P, RB], F32, name="sel32f", tag="sel32f")
+        nc.vector.tensor_reduce(out=sel32f[:], in_=ident_f[:].rearrange("p (r h) -> p r h", h=4), axis=AX.X, op=ALU.add)
+        sel32 = const.tile([P, RB], BF16, name="sel32", tag="sel32")
+        nc.vector.tensor_copy(out=sel32[:], in_=sel32f[:])
 
-        small = psum.tile([P, 32 * JT + JT], F32, name="small", tag="small", bufs=1)
+        small = psum.tile([P, 16 * JT + JT], F32, name="small", tag="small", bufs=1)
         bc = keep.tile([P, G, N], U32, name="bc", tag="bc", align_bytes=64)
         bs = keep.tile([P, G, N], U8, name="bs", tag="bs", align_bytes=64)
         xc = []
@@ -106,7 +124,7 @@ def tile_advresnet_kernel(tc, x, y, beta, bias_lin, W1, W2, bias1, bias2, adv, o
         o = keep.tile([P, BT, N], F32, name="o", tag="o")
         o8 = keep.tile([P, BT, N], FP8, name="o8", tag="o8")
         bnb = keep.tile([P, N], F32, name="bnb", tag="bnb")
-        cbb = keep.tile([P, HALF], F32, name="cbb", tag="cbb")
+        psb = keep.tile([P, (JT - NT) * P], F32, name="psb", tag="psb")
         bnv = const.tile([P, JT], F32, name="bnv", tag="bnv")
         cb = const.tile([P, JT], F32, name="cb", tag="cb")
         sv = const.tile([P, JT], F32, name="sv", tag="sv")
@@ -114,38 +132,32 @@ def tile_advresnet_kernel(tc, x, y, beta, bias_lin, W1, W2, bias1, bias2, adv, o
         nc.vector.memset(ss[:], 0.0)
         cv = const.tile([P, JT], F32, name="cv", tag="cv")
         pm = const.tile([P, BT, len(BLOCKS)], F32, name="pm", tag="pm")
-        am = const.tile([P, BT], F32, name="am", tag="am")
+        m1 = const.tile([P, BT], F32, name="m1", tag="m1")
         rs = const.tile([P, BT], F32, name="rs", tag="rs")
         r0 = const.tile([P, BT], F32, name="r0", tag="r0")
         r1 = const.tile([P, BT], F32, name="r1", tag="r1")
-        junk = const.tile([P, HALF], BF16, name="junk", tag="junk")
 
         abt = {}
         grps = {}
         xgs = {}
         accs = {}
         sps = {}
+        parts = {}
 
         def beta_abs(g, ci):
             if ci == 0:
                 ab = work.tile([P, 4, N], BF16, name="ab", tag="ab", bufs=2)
                 abt[g] = ab
             c0, c1, r = raw[g][ci]
-            nc.vector.tensor_scalar(out=abt[g][:, :, c0:c1], in0=r[:], scalar1=0.0, scalar2=None, op0=ALU.max)
+            nc.vector.tensor_scalar(out=abt[g][:, :, c0:c1].bitcast(I32), in0=r[:].bitcast(I32), scalar1=0x7FFF7FFF,
+                                    scalar2=None, op0=ALU.bitwise_and)
 
         def beta_norm_part(g):
             for t in range(4):
                 for jt in range(JT):
                     col = (g * 4 + t) * JT + jt
-                    for l0, l1, r in raw[g]:
-                        if l0 <= P * jt and P * (jt + 1) <= l1:
-                            nc.tensor.matmul(out=small[:, col:col + 1], lhsT=r[:, t, P * jt - l0:P * (jt + 1) - l0],
-                                             rhs=neg_b[:, 0:1], start=True, stop=True)
-            for t in range(4):
-                for jt in range(JT):
-                    col = (16 + g * 4 + t) * JT + jt
                     nc.tensor.matmul(out=small[:, col:col + 1], lhsT=abt[g][:, t, P * jt:P * (jt + 1)],
-                                     rhs=two_b[:, 0:1], start=True, stop=True)
+                                     rhs=one_b[:, 0:1], start=True, stop=True)
 
         def beta_copy(g, pi):
             if g not in grps:
@@ -184,7 +196,7 @@ def tile_advresnet_kernel(tc, x, y, beta, bias_lin, W1, W2, bias1, bias2, adv, o
                                   in_=xgs[bt][:].rearrange("p g b t -> p (g b t)"))
 
         def norm_reduce():
-            nc.vector.tensor_reduce(out=bnv[:], in_=small[:, 0:32 * JT].rearrange("p (s j) -> p j s", j=JT),
+            nc.vector.tensor_reduce(out=bnv[:], in_=small[:, 0:16 * JT].rearrange("p (s j) -> p j s", j=JT),
                                     axis=AX.X, op=ALU.add)
 
         def norm_spread(h):
@@ -221,38 +233,51 @@ def tile_advresnet_kernel(tc, x, y, beta, bias_lin, W1, W2, bias1, bias2, adv, o
             nc.vector.tensor_scalar(out=wv[:], in0=wv[:], scalar1=4096.0, scalar2=cb[:, t:t + 1],
                                     op0=ALU.mult, op1=ALU.add, accum_out=sv[:, t:t + 1])
 
-        def w2_tensor(t):
-            wp = w2[t][2]
-            wacc = psum.tile([P, HALF], F32, name="xt", tag="xt", bufs=2)
-            nch = PLAN[t][2] // HALF
-            for c in range(nch):
-                nc.tensor.matmul(out=wacc[:], lhsT=ident_b[:], rhs=wp[:, HALF * c:HALF * (c + 1)],
-                                 start=(c == 0), stop=(c == nch - 1))
-            nc.scalar.activation(out=junk[:], in_=wacc[:], func=ACT.Copy, scale=4096.0, accum_out=ss[:, t:t + 1])
-
         def const_spread(bi):
-            t0, nt, who = BLOCKS[bi]
+            t0, nt = BLOCKS[bi]
             nc.vector.tensor_tensor(out=cv[:, t0:t0 + nt], in0=sv[:, t0:t0 + nt], in1=ss[:, t0:t0 + nt], op=ALU.add)
-            sp = psum.tile([P, HALF], F32, name="xt", tag="xt", bufs=2)
+            sp = psum.tile([P, HALF], F32, name="acc", tag="acc", bufs=5)
             sps[bi] = sp
             for q in range(nt):
                 nc.tensor.transpose(out=sp[:, P * q:P * (q + 1)], in_=cv[:, t0 + q:t0 + q + 1].to_broadcast([P, P]),
                                     identity=ident_f[:])
 
+        def chunk_sum(bi, c):
+            t0, nt = BLOCKS[bi]
+            first = (t0 - NT) * P // RB
+            if c == first:
+                part = psum.tile([P, HALF], F32, name="xt", tag="xt", bufs=2)
+                parts[bi] = part
+            col = RB * (c - first)
+            for i in range(QW // P):
+                nc.tensor.matmul(out=parts[bi][:, col:col + RB], lhsT=wq[c][:, P * i:P * (i + 1)], rhs=sel32[:],
+                                 start=(i == 0), stop=(i == QW // P - 1))
+
+        def block_chunks(bi):
+            t0, nt = BLOCKS[bi]
+            return range((t0 - NT) * P // RB, (t0 + nt - NT) * P // RB)
+
+        def part_out(bi):
+            t0, nt = BLOCKS[bi]
+            off = P * (t0 - NT)
+            nc.scalar.activation(out=psb[:, off:off + P * nt], in_=parts[bi][:, 0:P * nt], func=ACT.Copy, scale=4096.0)
+
+        def part_join(bi):
+            t0, nt = BLOCKS[bi]
+            sp = psum.tile([P, HALF], F32, name="acc", tag="acc", bufs=5)
+            sps[bi] = sp
+            for q in range(nt):
+                off = P * (t0 + q - NT)
+                nc.tensor.matmul(out=sp[:, P * q:P * (q + 1)], lhsT=sel[:, t0 + q:t0 + q + 1].to_broadcast([P, P]),
+                                 rhs=brow[:], start=True, stop=False)
+                nc.tensor.matmul(out=sp[:, P * q:P * (q + 1)], lhsT=ones_f[:], rhs=psb[:, off:off + P],
+                                 start=False, stop=True)
+
         def block_cols(bi):
-            t0, nt, who = BLOCKS[bi]
+            t0, nt = BLOCKS[bi]
             return slice(P * t0, P * (t0 + nt)), nt * P
 
-        def const_add_gpsimd_prepare(bi):
-            js, w = block_cols(bi)
-            nc.scalar.copy(out=cbb[:, 0:w], in_=sps[bi][:, 0:w])
-
-        def const_add_gpsimd(bi, bt):
-            js, w = block_cols(bi)
-            nc.gpsimd.tensor_tensor(out=o[:, bt, js], in0=o[:, bt, js], in1=cbb[:, 0:w], op=ALU.add)
-            nc.sync.dma_start(out=out_0[P * bt:P * (bt + 1), js], in_=o[:, bt, js])
-
-        def const_add_vector(bi):
+        def const_add(bi):
             js, w = block_cols(bi)
             nc.vector.tensor_tensor(out=o[:, :, js], in0=o[:, :, js],
                                     in1=sps[bi][:, 0:w].unsqueeze(1).to_broadcast([P, BT, w]), op=ALU.add)
@@ -285,9 +310,9 @@ def tile_advresnet_kernel(tc, x, y, beta, bias_lin, W1, W2, bias1, bias2, adv, o
             beta_quant(1)
             beta_copy(2, 0)
             beta_copy(2, 1)
-            nc.tensor.matmul(out=small[:, 32 * JT:33 * JT], lhsT=brow[:], rhs=sel[:], start=True, stop=True)
-            nc.vector.tensor_copy(out=cb[:], in_=small[:, 32 * JT:33 * JT])
-            nc.vector.tensor_copy(out=sv[:], in_=small[:, 32 * JT:33 * JT])
+            nc.tensor.matmul(out=small[:, 16 * JT:17 * JT], lhsT=brow[:], rhs=sel[:], start=True, stop=True)
+            nc.vector.tensor_copy(out=cb[:], in_=small[:, 16 * JT:17 * JT])
+            nc.vector.tensor_copy(out=sv[:], in_=small[:, 16 * JT:17 * JT])
             norm_reduce()
             beta_copy(3, 1)
             x_turn(0)
@@ -325,29 +350,41 @@ def tile_advresnet_kernel(tc, x, y, beta, bias_lin, W1, W2, bias1, bias2, adv, o
             product(3, 1)
             add_y_term(3, 0)
             add_y_term(3, 1)
-            w2_tensor(4)
+            for c in range(0, 4):
+                chunk_sum(1, c)
             const_spread(0)
-            const_add_gpsimd_prepare(0)
-            w2_tensor(5)
-            for bt in range(BT):
-                const_add_gpsimd(0, bt)
-            w2_vector(5)
-            w2_vector(6)
-            w2_scalar(7)
-            w2_vector(7)
+            for c in range(4, 8):
+                chunk_sum(1, c)
+            const_add(0)
+            part_out(1)
+            part_join(1)
+            for c in block_chunks(2):
+                chunk_sum(2, c)
             row_max(0, 0)
-            const_spread(1)
             row_max(0, 1)
-            const_add_vector(1)
+            const_add(1)
+            part_out(2)
+            part_join(2)
+            for c in block_chunks(3):
+                chunk_sum(3, c)
             row_max(0, 2)
-            row_max(1, 0)
-            row_max(1, 1)
             row_max(0, 3)
-            nc.vector.reciprocal(out=r0[:], in_=pm[:, :, 0])
-            row_max(1, 2)
-            row_max(1, 3)
+            const_add(2)
+            part_out(3)
+            part_join(3)
+            for bt in range(BT):
+                row_max(1, bt)
+            const_add(3)
+            for bt in range(BT):
+                row_max(2, bt)
+            row_max(3, 0)
+            nc.vector.tensor_reduce(out=m1[:], in_=pm[:, :, 0:3], axis=AX.X, op=ALU.max)
+            row_max(3, 1)
+            nc.vector.reciprocal(out=r0[:], in_=m1[:])
+            row_max(3, 2)
             nc.vector.tensor_scalar(out=r0[:], in0=r0[:], scalar1=448.0, scalar2=None, op0=ALU.mult)
-            nc.vector.reciprocal(out=r1[:], in_=pm[:, :, 1])
+            row_max(3, 3)
+            nc.vector.reciprocal(out=r1[:], in_=pm[:, :, 3])
             nc.vector.scalar_tensor_tensor(out=rs[:], in0=r1[:], scalar=448.0, in1=r0[:], op0=ALU.mult, op1=ALU.min)
             for bt in (3, 0, 1, 2):
                 if bt == 3:

@@ -55,13 +55,13 @@ def tile_advresnet_kernel(tc, x, y, beta, bias_lin, W1, W2, bias1, bias2, adv, o
                 nc.sync.dma_start(out=r[:], in_=rows[:, :, c0:c1])
                 chunks.append((c0, c1, r))
             raw.append(chunks)
-        y_sb = keep.tile([P, BT, N], BF16, name="y_sb", tag="y_sb")
-        nc.sync.dma_start(out=y_sb[:], in_=y.rearrange("(t p) c -> p t c", p=P))
         x_sb = []
         for bt in range(BT):
             xl = keep.tile([P, K], BF16, name="x_sb%d" % bt, tag="x_sb%d" % bt)
             nc.sync.dma_start(out=xl[:], in_=x[P * bt:P * (bt + 1), :])
             x_sb.append(xl)
+        y_sb = keep.tile([P, BT, N], BF16, name="y_sb", tag="y_sb")
+        nc.sync.dma_start(out=y_sb[:], in_=y.rearrange("(t p) c -> p t c", p=P))
         w2 = []
         for t in range(NT):
             rows = W2[P * t:P * (t + 1), :]
@@ -182,7 +182,7 @@ def tile_advresnet_kernel(tc, x, y, beta, bias_lin, W1, W2, bias1, bias2, adv, o
             xg = work.tile([P, G, P, 4], BF16, name="xg", tag="xg", bufs=3, align_bytes=64)
             xgs[bt] = xg
             for gp in range(G // 2):
-                xt = psum.tile([P, 2, 2, P], F32, name="xt", tag="xt", bufs=2)
+                xt = psum.tile([P, 2, 2, P], F32, name="bank", tag="bank", bufs=7)
                 for g2 in range(2):
                     g = 2 * gp + g2
                     for u in range(2):
@@ -200,7 +200,7 @@ def tile_advresnet_kernel(tc, x, y, beta, bias_lin, W1, W2, bias1, bias2, adv, o
                                     axis=AX.X, op=ALU.add)
 
         def norm_spread(h):
-            sp = psum.tile([P, HALF], F32, name="acc", tag="acc", bufs=5)
+            sp = psum.tile([P, HALF], F32, name="bank", tag="bank", bufs=7)
             for q in range(4):
                 jt = 4 * h + q
                 nc.tensor.transpose(out=sp[:, P * q:P * (q + 1)], in_=bnv[:, jt:jt + 1].to_broadcast([P, P]),
@@ -212,7 +212,7 @@ def tile_advresnet_kernel(tc, x, y, beta, bias_lin, W1, W2, bias1, bias2, adv, o
 
         def product(bt, h):
             hs = slice(HALF * h, HALF * (h + 1))
-            acc = psum.tile([P, HALF], F32, name="acc", tag="acc", bufs=5)
+            acc = psum.tile([P, HALF], F32, name="bank", tag="bank", bufs=7)
             accs[(bt, h)] = acc
             for g in range(G):
                 gs = slice(P * g, P * (g + 1))
@@ -236,7 +236,7 @@ def tile_advresnet_kernel(tc, x, y, beta, bias_lin, W1, W2, bias1, bias2, adv, o
         def const_spread(bi):
             t0, nt = BLOCKS[bi]
             nc.vector.tensor_tensor(out=cv[:, t0:t0 + nt], in0=sv[:, t0:t0 + nt], in1=ss[:, t0:t0 + nt], op=ALU.add)
-            sp = psum.tile([P, HALF], F32, name="acc", tag="acc", bufs=5)
+            sp = psum.tile([P, HALF], F32, name="bank", tag="bank", bufs=7)
             sps[bi] = sp
             for q in range(nt):
                 nc.tensor.transpose(out=sp[:, P * q:P * (q + 1)], in_=cv[:, t0 + q:t0 + q + 1].to_broadcast([P, P]),
@@ -246,7 +246,7 @@ def tile_advresnet_kernel(tc, x, y, beta, bias_lin, W1, W2, bias1, bias2, adv, o
             t0, nt = BLOCKS[bi]
             first = (t0 - NT) * P // RB
             if c == first:
-                part = psum.tile([P, HALF], F32, name="xt", tag="xt", bufs=2)
+                part = psum.tile([P, HALF], F32, name="bank", tag="bank", bufs=7)
                 parts[bi] = part
             col = RB * (c - first)
             for i in range(QW // P):
@@ -264,12 +264,12 @@ def tile_advresnet_kernel(tc, x, y, beta, bias_lin, W1, W2, bias1, bias2, adv, o
 
         def part_join(bi):
             t0, nt = BLOCKS[bi]
-            sp = psum.tile([P, HALF], F32, name="acc", tag="acc", bufs=5)
+            sp = psum.tile([P, HALF], F32, name="bank", tag="bank", bufs=7)
             sps[bi] = sp
             for q in range(nt):
                 off = P * (t0 + q - NT)
-                nc.tensor.matmul(out=sp[:, P * q:P * (q + 1)], lhsT=sel[:, t0 + q:t0 + q + 1].to_broadcast([P, P]),
-                                 rhs=brow[:], start=True, stop=False)
+                nc.tensor.matmul(out=sp[:, P * q:P * (q + 1)], lhsT=cb[:, t0 + q:t0 + q + 1].to_broadcast([P, P]),
+                                 rhs=ident_f[:], is_transpose=True, start=True, stop=False)
                 nc.tensor.matmul(out=sp[:, P * q:P * (q + 1)], lhsT=ones_f[:], rhs=psb[:, off:off + P],
                                  start=False, stop=True)
 

@@ -27,9 +27,9 @@ BYTES = 2 * (B * K + B * N + K * N + N * NH + 2 * N) + 5 * B * N
 CV = 512
 PARTS0 = ((0, 256, "v"), (256, 512, "s"), (512, 768, "v"), (768, 1024, "s"))
 PARTS = ((0, CV, "v"), (CV, N, "s"))
-PLAN = ((0, NH), (NH, 0), (0, NH), (NH, 0))
+PLAN = ((NH, 0), (0, NH), (NH, 0))
 NT = len(PLAN)
-BLOCKS = ((0, 4), (4, 2), (6, 1), (7, 1))
+BLOCKS = ((0, 3), (3, 2), (5, 2), (7, 1))
 RB = 32
 QW = NH // 4
 NCH = (JT - NT) * P // RB
@@ -330,16 +330,15 @@ def tile_advresnet_kernel(tc, x, y, beta, bias_lin, W1, W2, bias1, bias2, adv, o
             x_quant(1)
             product(0, 0)
             product(0, 1)
-            w2_vector(0)
             x_quant(2)
             x_quant(3)
-            w2_scalar(1)
+            w2_vector(1)
+            w2_scalar(0)
             add_y_term(0, 0)
             add_y_term(0, 1)
             product(1, 0)
             product(1, 1)
-            w2_vector(2)
-            w2_scalar(3)
+            w2_scalar(2)
             add_y_term(1, 0)
             add_y_term(1, 1)
             product(2, 0)

@@ -27,9 +27,9 @@ BYTES = 2 * (B * K + B * N + K * N + N * NH + 2 * N) + 5 * B * N
 CV = 512
 PARTS0 = ((0, 256, "v"), (256, 512, "s"), (512, 768, "v"), (768, 1024, "s"))
 PARTS = ((0, CV, "v"), (CV, N, "s"))
-PLAN = ((NH, 0), (0, NH), (NH, 0))
+PLAN = ((NH, 0), (0, NH), (2688, NH - 2688))
 NT = len(PLAN)
-BLOCKS = ((0, 3), (3, 2), (5, 2), (7, 1))
+BLOCKS = ((0, 3), (3, 2), (5, 1), (6, 1), (7, 1))
 RB = 32
 QW = NH // 4
 NCH = (JT - NT) * P // RB
@@ -233,9 +233,12 @@ def tile_advresnet_kernel(tc, x, y, beta, bias_lin, W1, W2, bias1, bias2, adv, o
             nc.vector.tensor_scalar(out=wv[:], in0=wv[:], scalar1=4096.0, scalar2=cb[:, t:t + 1],
                                     op0=ALU.mult, op1=ALU.add, accum_out=sv[:, t:t + 1])
 
-        def const_spread(bi):
+        def const_join(bi):
             t0, nt = BLOCKS[bi]
             nc.vector.tensor_tensor(out=cv[:, t0:t0 + nt], in0=sv[:, t0:t0 + nt], in1=ss[:, t0:t0 + nt], op=ALU.add)
+
+        def const_spread(bi):
+            t0, nt = BLOCKS[bi]
             sp = psum.tile([P, HALF], F32, name="bank", tag="bank", bufs=7)
             sps[bi] = sp
             for q in range(nt):
@@ -341,6 +344,7 @@ def tile_advresnet_kernel(tc, x, y, beta, bias_lin, W1, W2, bias1, bias2, adv, o
             w2_scalar(2)
             add_y_term(1, 0)
             add_y_term(1, 1)
+            w2_vector(2)
             product(2, 0)
             product(2, 1)
             add_y_term(2, 0)
@@ -348,6 +352,7 @@ def tile_advresnet_kernel(tc, x, y, beta, bias_lin, W1, W2, bias1, bias2, adv, o
             product(3, 0)
             product(3, 1)
             add_y_term(3, 0)
+            const_join(0)
             add_y_term(3, 1)
             for c in range(0, 4):
                 chunk_sum(1, c)
@@ -356,34 +361,47 @@ def tile_advresnet_kernel(tc, x, y, beta, bias_lin, W1, W2, bias1, bias2, adv, o
                 chunk_sum(1, c)
             const_add(0)
             part_out(1)
-            part_join(1)
-            for c in block_chunks(2):
+            for c in range(8, 12):
                 chunk_sum(2, c)
+            part_join(1)
+            part_out(2)
             row_max(0, 0)
             row_max(0, 1)
             const_add(1)
-            part_out(2)
+            chunk_sum(3, 12)
+            chunk_sum(3, 13)
             part_join(2)
-            for c in block_chunks(3):
-                chunk_sum(3, c)
+            chunk_sum(3, 14)
+            chunk_sum(3, 15)
+            part_out(3)
             row_max(0, 2)
             row_max(0, 3)
             const_add(2)
-            part_out(3)
+            chunk_sum(4, 16)
+            chunk_sum(4, 17)
             part_join(3)
+            chunk_sum(4, 18)
+            chunk_sum(4, 19)
+            part_out(4)
+            part_join(4)
             for bt in range(BT):
                 row_max(1, bt)
             const_add(3)
             for bt in range(BT):
                 row_max(2, bt)
             row_max(3, 0)
-            nc.vector.tensor_reduce(out=m1[:], in_=pm[:, :, 0:3], axis=AX.X, op=ALU.max)
             row_max(3, 1)
-            nc.vector.reciprocal(out=r0[:], in_=m1[:])
+            const_add(4)
             row_max(3, 2)
-            nc.vector.tensor_scalar(out=r0[:], in0=r0[:], scalar1=448.0, scalar2=None, op0=ALU.mult)
             row_max(3, 3)
-            nc.vector.reciprocal(out=r1[:], in_=pm[:, :, 3])
+            row_max(4, 0)
+            nc.vector.tensor_reduce(out=m1[:], in_=pm[:, :, 0:4], axis=AX.X, op=ALU.max)
+            row_max(4, 1)
+            nc.vector.reciprocal(out=r0[:], in_=m1[:])
+            row_max(4, 2)
+            nc.vector.tensor_scalar(out=r0[:], in0=r0[:], scalar1=448.0, scalar2=None, op0=ALU.mult)
+            row_max(4, 3)
+            nc.vector.reciprocal(out=r1[:], in_=pm[:, :, 4])
             nc.vector.scalar_tensor_tensor(out=rs[:], in0=r1[:], scalar=448.0, in1=r0[:], op0=ALU.mult, op1=ALU.min)
             for bt in (3, 0, 1, 2):
                 if bt == 3:

@@ -27,6 +27,7 @@ BYTES = 2 * (B * K + B * N + K * N + N * NH + 2 * N) + 5 * B * N
 CV = 512
 PARTS0 = ((0, 256, "v"), (256, 512, "s"), (512, 768, "v"), (768, 1024, "s"))
 PARTS = ((0, CV, "v"), (CV, N, "s"))
+CUTS0 = ((0, 512, "-"), (512, 1024, "-"))
 PLAN = ((NH, 0), (0, NH), (2688, NH - 2688))
 NT = len(PLAN)
 BLOCKS = ((0, 3), (3, 2), (5, 1), (6, 1), (7, 1))
@@ -48,34 +49,28 @@ def tile_advresnet_kernel(tc, x, y, beta, bias_lin, W1, W2, bias1, bias2, adv, o
         for g in range(G):
             rows = beta[512 * g:512 * (g + 1), :].rearrange("(p t) c -> p t c", t=4)
             chunks = []
-            cuts = PARTS0 if g == 0 else ((0, N, "-"),)
+            cuts = CUTS0 if g == 0 else ((0, N, "-"),)
             for ci in range(len(cuts)):
                 c0, c1, who = cuts[ci]
                 r = keep.tile([P, 4, c1 - c0], BF16, name="raw%d_%d" % (g, ci), tag="raw%d_%d" % (g, ci))
                 nc.sync.dma_start(out=r[:], in_=rows[:, :, c0:c1])
                 chunks.append((c0, c1, r))
             raw.append(chunks)
+        x_rows = x.rearrange("(p t) k -> p t k", t=BT)
         x_sb = []
-        for bt in range(BT):
-            xl = keep.tile([P, K], BF16, name="x_sb%d" % bt, tag="x_sb%d" % bt)
-            nc.sync.dma_start(out=xl[:], in_=x[P * bt:P * (bt + 1), :])
-            x_sb.append(xl)
+        for h in range(BT // 2):
+            xl = keep.tile([P, 2, K], BF16, name="x_sb%d" % h, tag="x_sb%d" % h)
+            nc.sync.dma_start(out=xl[:], in_=x_rows[:, 2 * h:2 * h + 2, :])
+            x_sb.append(xl[:, 0, :])
+            x_sb.append(xl[:, 1, :])
         y_sb = keep.tile([P, BT, N], BF16, name="y_sb", tag="y_sb")
-        nc.sync.dma_start(out=y_sb[:], in_=y.rearrange("(t p) c -> p t c", p=P))
+        nc.sync.dma_start(out=y_sb[:], in_=y.rearrange("(p t) c -> p t c", t=BT))
         w2 = []
         for t in range(NT):
-            rows = W2[P * t:P * (t + 1), :]
-            tiles = []
-            c0 = 0
-            for k in range(2):
-                n = PLAN[t][k]
-                wt = None
-                if n > 0:
-                    wt = keep.tile([P, n], BF16, name="w2_%d_%d" % (t, k), tag="w2_%d_%d" % (t, k))
-                    nc.sync.dma_start(out=wt[:], in_=rows[:, c0:c0 + n])
-                tiles.append(wt)
-                c0 += n
-            w2.append(tiles)
+            wt = keep.tile([P, NH], BF16, name="w2_%d" % t, tag="w2_%d" % t)
+            nc.sync.dma_start(out=wt[:], in_=W2[P * t:P * (t + 1), :])
+            cut = PLAN[t][0]
+            w2.append((wt[:, 0:cut] if cut > 0 else None, wt[:, cut:NH] if cut < NH else None))
         quarters = W2.rearrange("j (h q) -> (j h) q", q=QW)
         wq = []
         for d in range(NCH // 4 - 1):
@@ -178,7 +173,7 @@ def tile_advresnet_kernel(tc, x, y, beta, bias_lin, W1, W2, bias1, bias2, adv, o
                                   in_=grps[g][:].rearrange("p c t -> p (c t)"))
 
         def x_turn(bt):
-            xw = x_sb[bt][:].bitcast(F32)
+            xw = x_sb[bt].bitcast(F32)
             xg = work.tile([P, G, P, 4], BF16, name="xg", tag="xg", bufs=3, align_bytes=64)
             xgs[bt] = xg
             for gp in range(G // 2):
@@ -226,11 +221,11 @@ def tile_advresnet_kernel(tc, x, y, beta, bias_lin, W1, W2, bias1, bias2, adv, o
 
         def w2_scalar(t):
             ws = w2[t][0]
-            nc.scalar.activation(out=ws[:], in_=ws[:], func=ACT.Copy, scale=4096.0, accum_out=ss[:, t:t + 1])
+            nc.scalar.activation(out=ws, in_=ws, func=ACT.Copy, scale=4096.0, accum_out=ss[:, t:t + 1])
 
         def w2_vector(t):
             wv = w2[t][1]
-            nc.vector.tensor_scalar(out=wv[:], in0=wv[:], scalar1=4096.0, scalar2=cb[:, t:t + 1],
+            nc.vector.tensor_scalar(out=wv, in0=wv, scalar1=4096.0, scalar2=cb[:, t:t + 1],
                                     op0=ALU.mult, op1=ALU.add, accum_out=sv[:, t:t + 1])
 
         def const_join(bi):
@@ -284,7 +279,7 @@ def tile_advresnet_kernel(tc, x, y, beta, bias_lin, W1, W2, bias1, bias2, adv, o
             js, w = block_cols(bi)
             nc.vector.tensor_tensor(out=o[:, :, js], in0=o[:, :, js],
                                     in1=sps[bi][:, 0:w].unsqueeze(1).to_broadcast([P, BT, w]), op=ALU.add)
-            nc.sync.dma_start(out=out_0.rearrange("(t p) c -> p t c", p=P)[:, :, js], in_=o[:, :, js])
+            nc.sync.dma_start(out=out_0.rearrange("(p t) c -> p t c", t=BT)[:, :, js], in_=o[:, :, js])
 
         def row_max(bi, bt):
             js, w = block_cols(bi)
@@ -292,14 +287,12 @@ def tile_advresnet_kernel(tc, x, y, beta, bias_lin, W1, W2, bias1, bias2, adv, o
                                     apply_absolute_value=True)
 
         with tc.manual_schedule():
-            beta_abs(0, 0)
             beta_copy(0, 0)
             beta_copy(0, 1)
-            beta_abs(0, 1)
-            beta_abs(0, 2)
+            beta_abs(0, 0)
             beta_copy(0, 2)
             beta_copy(0, 3)
-            beta_abs(0, 3)
+            beta_abs(0, 1)
             beta_norm_part(0)
             beta_quant(0)
             beta_abs(1, 0)
@@ -410,4 +403,4 @@ def tile_advresnet_kernel(tc, x, y, beta, bias_lin, W1, W2, bias1, bias2, adv, o
                 else:
                     nc.vector.tensor_scalar(out=o8[:, bt, :], in0=o[:, bt, :], scalar1=rs[:, bt:bt + 1], scalar2=None,
                                             op0=ALU.mult, saturate=False)
-                nc.sync.dma_start(out=out_1[P * bt:P * (bt + 1), :], in_=o8[:, bt, :].bitcast(U8))
+                nc.sync.dma_start(out=out_1.rearrange("(p t) c -> p t c", t=BT)[:, bt, :], in_=o8[:, bt, :].bitcast(U8))

@@ -25,9 +25,7 @@ FLOPS = 2 * B * K * N
 BYTES = 2 * (B * K + B * N + K * N + N * NH + 2 * N) + 5 * B * N
 
 CV = 512
-PARTS0 = ((0, 256, "v"), (256, 512, "s"), (512, 768, "v"), (768, 1024, "s"))
 PARTS = ((0, CV, "v"), (CV, N, "s"))
-CUTS0 = ((0, 512, "-"), (512, 1024, "-"))
 PLAN = ((NH, 0), (0, NH), (2688, NH - 2688))
 NT = len(PLAN)
 BLOCKS = ((0, 3), (3, 2), (5, 1), (6, 1), (7, 1))
@@ -49,7 +47,7 @@ def tile_advresnet_kernel(tc, x, y, beta, bias_lin, W1, W2, bias1, bias2, adv, o
         for g in range(G):
             rows = beta[512 * g:512 * (g + 1), :].rearrange("(p t) c -> p t c", t=4)
             chunks = []
-            cuts = CUTS0 if g == 0 else ((0, N, "-"),)
+            cuts = ((0, N, "-"),)
             for ci in range(len(cuts)):
                 c0, c1, who = cuts[ci]
                 r = keep.tile([P, 4, c1 - c0], BF16, name="raw%d_%d" % (g, ci), tag="raw%d_%d" % (g, ci))
@@ -158,7 +156,7 @@ def tile_advresnet_kernel(tc, x, y, beta, bias_lin, W1, W2, bias1, bias2, adv, o
             if g not in grps:
                 grp = work.tile([P, N, 4], BF16, name="grp", tag="grp", bufs=3, align_bytes=64)
                 grps[g] = grp
-            c0, c1, who = (PARTS0 if g == 0 else PARTS)[pi]
+            c0, c1, who = PARTS[pi]
             for l0, l1, r in raw[g]:
                 if l0 <= c0 and c1 <= l1:
                     src = r[:, :, c0 - l0:c1 - l0].rearrange("p t (c i) -> p c t i", i=4)
@@ -290,9 +288,6 @@ def tile_advresnet_kernel(tc, x, y, beta, bias_lin, W1, W2, bias1, bias2, adv, o
             beta_copy(0, 0)
             beta_copy(0, 1)
             beta_abs(0, 0)
-            beta_copy(0, 2)
-            beta_copy(0, 3)
-            beta_abs(0, 1)
             beta_norm_part(0)
             beta_quant(0)
             beta_abs(1, 0)

@@ -388,14 +388,29 @@ def tile_advresnet_kernel(tc, x, y, beta, bias_lin, W1, W2, bias1, bias2, adv, o
             nc.vector.reciprocal(out=r0[:], in_=m1[:])
             row_max(4, 2)
             nc.vector.tensor_scalar(out=r0[:], in0=r0[:], scalar1=448.0, scalar2=None, op0=ALU.mult)
-            row_max(4, 3)
-            nc.vector.reciprocal(out=r1[:], in_=pm[:, :, 4])
-            nc.vector.scalar_tensor_tensor(out=rs[:], in0=r1[:], scalar=448.0, in1=r0[:], op0=ALU.mult, op1=ALU.min)
-            for bt in (3, 0, 1, 2):
-                if bt == 3:
+
+            def last_reciprocal(b0, b1):
+                nc.vector.reciprocal(out=r1[:, b0:b1], in_=pm[:, b0:b1, 4])
+
+            def factor(b0, b1):
+                nc.vector.scalar_tensor_tensor(out=rs[:, b0:b1], in0=r1[:, b0:b1], scalar=448.0, in1=r0[:, b0:b1],
+                                               op0=ALU.mult, op1=ALU.min)
+
+            def cast(bt, who):
+                if who == "s":
                     nc.scalar.activation(out=o8[:, bt, :], in_=o[:, bt, :], func=ACT.Identity, scale=rs[:, bt:bt + 1],
                                          bias=zeros[:, 0:1], saturate=False)
                 else:
                     nc.vector.tensor_scalar(out=o8[:, bt, :], in0=o[:, bt, :], scalar1=rs[:, bt:bt + 1], scalar2=None,
                                             op0=ALU.mult, saturate=False)
                 nc.sync.dma_start(out=out_1.rearrange("(p t) c -> p t c", t=BT)[:, bt, :], in_=o8[:, bt, :].bitcast(U8))
+
+            last_reciprocal(0, 2)
+            row_max(4, 3)
+            factor(0, 2)
+            last_reciprocal(2, 4)
+            cast(0, "s")
+            cast(1, "v")
+            factor(2, 4)
+            cast(2, "v")
+            cast(3, "v")

@@ -244,9 +244,15 @@ def tile_advresnet_kernel(tc, x, y, beta, bias_lin, W1, W2, bias1, bias2, adv, o
             if c == first:
                 part = psum.tile([P, HALF], F32, name="bank", tag="bank", bufs=7)
                 parts[bi] = part
+            dst = parts[bi]
             col = RB * (c - first)
+            if c == NCH - 1:
+                last = psum.tile([P, HALF], F32, name="bank", tag="bank", bufs=7)
+                parts["last"] = last
+                dst = last
+                col = 0
             for i in range(QW // P):
-                nc.tensor.matmul(out=parts[bi][:, col:col + RB], lhsT=wq[c][:, P * i:P * (i + 1)], rhs=sel32[:],
+                nc.tensor.matmul(out=dst[:, col:col + RB], lhsT=wq[c][:, P * i:P * (i + 1)], rhs=sel32[:],
                                  start=(i == 0), stop=(i == QW // P - 1))
 
         def block_chunks(bi):
@@ -268,6 +274,27 @@ def tile_advresnet_kernel(tc, x, y, beta, bias_lin, W1, W2, bias1, bias2, adv, o
                                  rhs=ident_f[:], is_transpose=True, start=True, stop=False)
                 nc.tensor.matmul(out=sp[:, P * q:P * (q + 1)], lhsT=ones_f[:], rhs=psb[:, off:off + P],
                                  start=False, stop=True)
+
+        LB = len(BLOCKS) - 1
+        LOFF = P * (JT - 1 - NT)
+        LW = P - RB
+
+        def last_out(step):
+            if step == 0:
+                nc.scalar.activation(out=psb[:, LOFF:LOFF + LW], in_=parts[LB][:, 0:LW], func=ACT.Copy, scale=4096.0)
+            else:
+                nc.scalar.activation(out=psb[:, LOFF + LW:LOFF + P], in_=parts["last"][:, 0:RB], func=ACT.Copy, scale=4096.0)
+
+        def last_join(step):
+            if step == 0:
+                sp = psum.tile([P, HALF], F32, name="bank", tag="bank", bufs=7)
+                sps[LB] = sp
+                nc.tensor.matmul(out=sp[:, 0:P], lhsT=cb[:, JT - 1:JT].to_broadcast([P, P]), rhs=ident_f[:],
+                                 is_transpose=True, start=True, stop=False)
+            elif step == 1:
+                nc.tensor.matmul(out=sps[LB][:, 0:LW], lhsT=ones_f[:], rhs=psb[:, LOFF:LOFF + LW], start=False, stop=False)
+            else:
+                nc.tensor.matmul(out=sps[LB][:, LW:P], lhsT=ones_f[:], rhs=psb[:, LOFF + LW:LOFF + P], start=False, stop=True)
 
         def block_cols(bi):
             t0, nt = BLOCKS[bi]
@@ -369,9 +396,12 @@ def tile_advresnet_kernel(tc, x, y, beta, bias_lin, W1, W2, bias1, bias2, adv, o
             chunk_sum(4, 17)
             part_join(3)
             chunk_sum(4, 18)
+            last_out(0)
+            last_join(0)
             chunk_sum(4, 19)
-            part_out(4)
-            part_join(4)
+            last_out(1)
+            last_join(1)
+            last_join(2)
             for bt in range(BT):
                 row_max(1, bt)
             const_add(3)

@@ -118,6 +118,7 @@ def tile_advresnet_kernel(tc, x, y, beta, bias_lin, W1, W2, bias1, bias2, adv, o
         o8 = keep.tile([P, BT, N], FP8, name="o8", tag="o8")
         bnb = keep.tile([P, N], F32, name="bnb", tag="bnb")
         psb = keep.tile([P, (JT - NT) * P], F32, name="psb", tag="psb")
+        csb = keep.tile([P, N], F32, name="csb", tag="csb")
         bnv = const.tile([P, JT], F32, name="bnv", tag="bnv")
         cb = const.tile([P, JT], F32, name="cb", tag="cb")
         sv = const.tile([P, JT], F32, name="sv", tag="sv")
@@ -306,6 +307,21 @@ def tile_advresnet_kernel(tc, x, y, beta, bias_lin, W1, W2, bias1, bias2, adv, o
                                     in1=sps[bi][:, 0:w].unsqueeze(1).to_broadcast([P, BT, w]), op=ALU.add)
             nc.sync.dma_start(out=out_0.rearrange("(p t) c -> p t c", t=BT)[:, :, js], in_=o[:, :, js])
 
+        def add_v(bi):
+            js, w = block_cols(bi)
+            nc.vector.tensor_tensor(out=o[:, 0:2, js], in0=o[:, 0:2, js],
+                                    in1=sps[bi][:, 0:w].unsqueeze(1).to_broadcast([P, 2, w]), op=ALU.add)
+
+        def add_s(bi):
+            js, w = block_cols(bi)
+            nc.scalar.copy(out=csb[:, js], in_=sps[bi][:, 0:w])
+
+        def add_g(bi):
+            js, w = block_cols(bi)
+            nc.gpsimd.tensor_tensor(out=o[:, 2:4, js], in0=o[:, 2:4, js],
+                                    in1=csb[:, js].unsqueeze(1).to_broadcast([P, 2, w]), op=ALU.add)
+            nc.sync.dma_start(out=out_0.rearrange("(p t) c -> p t c", t=BT)[:, :, js], in_=o[:, :, js])
+
         def row_max(bi, bt):
             js, w = block_cols(bi)
             nc.vector.tensor_reduce(out=pm[:, bt, bi:bi + 1], in_=o[:, bt, js], axis=AX.X, op=ALU.max,
@@ -382,16 +398,22 @@ def tile_advresnet_kernel(tc, x, y, beta, bias_lin, W1, W2, bias1, bias2, adv, o
             part_out(2)
             row_max(0, 0)
             row_max(0, 1)
-            const_add(1)
+            row_max(0, 2)
+            add_v(1)
+            add_s(1)
+            add_g(1)
             chunk_sum(3, 12)
             chunk_sum(3, 13)
             part_join(2)
             chunk_sum(3, 14)
             chunk_sum(3, 15)
             part_out(3)
-            row_max(0, 2)
             row_max(0, 3)
-            const_add(2)
+            row_max(1, 0)
+            row_max(1, 1)
+            add_v(2)
+            add_s(2)
+            add_g(2)
             chunk_sum(4, 16)
             chunk_sum(4, 17)
             part_join(3)
@@ -402,13 +424,17 @@ def tile_advresnet_kernel(tc, x, y, beta, bias_lin, W1, W2, bias1, bias2, adv, o
             last_out(1)
             last_join(1)
             last_join(2)
-            for bt in range(BT):
-                row_max(1, bt)
-            const_add(3)
-            for bt in range(BT):
-                row_max(2, bt)
+            row_max(2, 0)
+            row_max(2, 1)
+            row_max(1, 2)
+            row_max(1, 3)
+            add_v(3)
+            add_s(3)
+            add_g(3)
             row_max(3, 0)
             row_max(3, 1)
+            row_max(2, 2)
+            row_max(2, 3)
             const_add(4)
             row_max(3, 2)
             row_max(3, 3)

from contextlib import ExitStack

import concourse.mybir as mybir
from concourse.masks import make_identity

F32 = mybir.dt.float32
BF16 = mybir.dt.bfloat16
I32 = mybir.dt.int32
U32 = mybir.dt.uint32
U8 = mybir.dt.uint8
FP8X4 = mybir.dt.float8_e4m3fn_x4
FP8 = mybir.dt.float8_e4m3fn
ALU = mybir.AluOpType
ACT = mybir.ActivationFunctionType
AX = mybir.AxisListType

B, K, NH, N = 512, 2048, 4096, 1024
P = 128
BT = B // P
G = K // 512
JT = N // P
HALF = 512

FLOPS = 2 * B * K * N
BYTES = 2 * (B * K + B * N + K * N + N * NH + 2 * N) + 5 * B * N

CV = 512
PARTS = ((0, CV, "v"), (CV, N, "s"))
PLAN = ((NH, 0), (0, NH), (2688, NH - 2688))
NT = len(PLAN)
BLOCKS = ((0, 3), (3, 2), (5, 1), (6, 1), (7, 1))
RB = 32
QW = NH // 4
NCH = (JT - NT) * P // RB


def tile_advresnet_kernel(tc, x, y, beta, bias_lin, W1, W2, bias1, bias2, adv, out_0, out_1):
    nc = tc.nc
    assert adv == 1
    with ExitStack() as ctx:
        const = ctx.enter_context(tc.tile_pool(name="const", bufs=1))
        keep = ctx.enter_context(tc.tile_pool(name="keep", bufs=1))
        work = ctx.enter_context(tc.tile_pool(name="work", bufs=2))
        psum = ctx.enter_context(tc.psum_pool(name="psum", bufs=2))

        raw = []
        for g in range(G):
            rows = beta[512 * g:512 * (g + 1), :].rearrange("(p t) c -> p t c", t=4)
            chunks = []
            cuts = ((0, N, "-"),)
            for ci in range(len(cuts)):
                c0, c1, who = cuts[ci]
                r = keep.tile([P, 4, c1 - c0], BF16, name="raw%d_%d" % (g, ci), tag="raw%d_%d" % (g, ci))
                nc.sync.dma_start(out=r[:], in_=rows[:, :, c0:c1])
                chunks.append((c0, c1, r))
            raw.append(chunks)
        x_rows = x.rearrange("(p t) k -> p t k", t=BT)
        x_sb = []
        for h in range(BT // 2):
            xl = keep.tile([P, 2, K], BF16, name="x_sb%d" % h, tag="x_sb%d" % h)
            nc.sync.dma_start(out=xl[:], in_=x_rows[:, 2 * h:2 * h + 2, :])
            x_sb.append(xl[:, 0, :])
            x_sb.append(xl[:, 1, :])
        y_sb = keep.tile([P, BT, N], BF16, name="y_sb", tag="y_sb")
        nc.sync.dma_start(out=y_sb[:], in_=y.rearrange("(p t) c -> p t c", t=BT))
        w2 = []
        for t in range(NT):
            wt = keep.tile([P, NH], BF16, name="w2_%d" % t, tag="w2_%d" % t)
            nc.sync.dma_start(out=wt[:], in_=W2[P * t:P * (t + 1), :])
            cut = PLAN[t][0]
            w2.append((wt[:, 0:cut] if cut > 0 else None, wt[:, cut:NH] if cut < NH else None))
        quarters = W2.rearrange("j (h q) -> (j h) q", q=QW)
        wq = []
        for d in range(NCH // 4 - 1):
            wt = keep.tile([P, 4, QW], BF16, name="wq%d" % d, tag="wq%d" % d)
            first = 4 * P * NT + 4 * P * d
            nc.sync.dma_start(out=wt[:], in_=quarters[first:first + 4 * P, :].rearrange("(c p) q -> p c q", p=P))
            for c in range(4):
                wq.append(wt[:, c, :])
        for c in range(NCH - 4, NCH):
            wt = keep.tile([P, QW], BF16, name="wql%d" % c, tag="wql%d" % c)
            first = 4 * P * NT + P * c
            nc.sync.dma_start(out=wt[:], in_=quarters[first:first + P, :])
            wq.append(wt[:])

        zeros = const.tile([P, 1], F32, name="zeros", tag="zeros")
        nc.vector.memset(zeros[:], 0.0)
        warm = const.tile([P, 1], F32, name="warm", tag="warm")
        nc.scalar.activation(out=warm[:], in_=zeros[:], func=ACT.Copy)
        one_b = const.tile([P, 1], BF16, name="one_b", tag="one_b")
        nc.vector.memset(one_b[:], 1.0)
        ones_f = const.tile([P, P], F32, name="ones_f", tag="ones_f")
        nc.vector.memset(ones_f[:], 1.0)
        brow = const.tile([P, P], BF16, name="brow", tag="brow")
        nc.vector.memset(brow[:], 0.0)
        nc.scalar.dma_start(out=brow[0:JT, :], in_=bias_lin.rearrange("(c p) -> c p", p=P))
        nc.scalar.dma_start(out=brow[JT:2 * JT, :], in_=bias2.rearrange("(c p) -> c p", p=P))
        ident_f = const.tile([P, P], F32, name="ident_f", tag="ident_f")
        make_identity(nc, ident_f[:])
        sel = const.tile([P, JT], BF16, name="sel", tag="sel")
        nc.vector.tensor_tensor(out=sel[:], in0=ident_f[:, 0:JT], in1=ident_f[:, JT:2 * JT], op=ALU.add)
        sel32f = const.tile([P, RB], F32, name="sel32f", tag="sel32f")
        nc.vector.tensor_reduce(out=sel32f[:], in_=ident_f[:].rearrange("p (r h) -> p r h", h=4), axis=AX.X, op=ALU.add)
        sel32 = const.tile([P, RB], BF16, name="sel32", tag="sel32")
        nc.vector.tensor_copy(out=sel32[:], in_=sel32f[:])

        small = psum.tile([P, 16 * JT + JT], F32, name="small", tag="small", bufs=1)
        bc = keep.tile([P, G, N], U32, name="bc", tag="bc", align_bytes=64)
        bs = keep.tile([P, G, N], U8, name="bs", tag="bs", align_bytes=64)
        xc = []
        xs = []
        for bt in range(BT):
            xct = keep.tile([P, G * P], U32, name="xc%d" % bt, tag="xc%d" % bt, align_bytes=64)
            xst = keep.tile([P, G * P], U8, name="xs%d" % bt, tag="xs%d" % bt, align_bytes=64)
            xc.append(xct)
            xs.append(xst)
        o = keep.tile([P, BT, N], F32, name="o", tag="o")
        o8 = keep.tile([P, BT, N], FP8, name="o8", tag="o8")
        bnb = keep.tile([P, N], F32, name="bnb", tag="bnb")
        psb = keep.tile([P, (JT - NT) * P], F32, name="psb", tag="psb")
        csb = keep.tile([P, N], F32, name="csb", tag="csb")
        bnv = const.tile([P, JT], F32, name="bnv", tag="bnv")
        cb = const.tile([P, JT], F32, name="cb", tag="cb")
        sv = const.tile([P, JT], F32, name="sv", tag="sv")
        ss = const.tile([P, JT], F32, name="ss", tag="ss")
        nc.vector.memset(ss[:], 0.0)
        cv = const.tile([P, JT], F32, name="cv", tag="cv")
        pm = const.tile([P, BT, len(BLOCKS)], F32, name="pm", tag="pm")
        m1 = const.tile([P, BT], F32, name="m1", tag="m1")
        rs = const.tile([P, BT], F32, name="rs", tag="rs")
        r0 = const.tile([P, BT], F32, name="r0", tag="r0")
        r1 = const.tile([P, BT], F32, name="r1", tag="r1")

        abt = {}
        grps = {}
        xgs = {}
        accs = {}
        sps = {}
        parts = {}

        def beta_abs(g, ci):
            if ci == 0:
                ab = work.tile([P, 4, N], BF16, name="ab", tag="ab", bufs=2)
                abt[g] = ab
            c0, c1, r = raw[g][ci]
            nc.vector.tensor_scalar(out=abt[g][:, :, c0:c1].bitcast(I32), in0=r[:].bitcast(I32), scalar1=0x7FFF7FFF,
                                    scalar2=None, op0=ALU.bitwise_and)

        def beta_norm_part(g):
            for t in range(4):
                for jt in range(JT):
                    col = (g * 4 + t) * JT + jt
                    nc.tensor.matmul(out=small[:, col:col + 1], lhsT=abt[g][:, t, P * jt:P * (jt + 1)],
                                     rhs=one_b[:, 0:1], start=True, stop=True)

        def beta_copy(g, pi):
            if g not in grps:
                grp = work.tile([P, N, 4], BF16, name="grp", tag="grp", bufs=3, align_bytes=64)
                grps[g] = grp
            c0, c1, who = PARTS[pi]
            for l0, l1, r in raw[g]:
                if l0 <= c0 and c1 <= l1:
                    src = r[:, :, c0 - l0:c1 - l0].rearrange("p t (c i) -> p c t i", i=4)
                    dst = grps[g][:, c0:c1, :].rearrange("p (c i) t -> p c t i", i=4)
                    if who == "v":
                        nc.vector.tensor_copy(out=dst, in_=src)
                    else:
                        nc.scalar.copy(out=dst, in_=src)

        def beta_quant(g):
            nc.vector.quantize_mx(out=bc[:, g, :].bitcast(FP8X4), scales=bs[:, g, :],
                                  in_=grps[g][:].rearrange("p c t -> p (c t)"))

        def x_turn(bt):
            xw = x_sb[bt].bitcast(F32)
            xg = work.tile([P, G, P, 4], BF16, name="xg", tag="xg", bufs=3, align_bytes=64)
            xgs[bt] = xg
            for gp in range(G // 2):
                xt = psum.tile([P, 2, 2, P], F32, name="bank", tag="bank", bufs=7)
                for g2 in range(2):
                    g = 2 * gp + g2
                    for u in range(2):
                        nc.tensor.transpose(out=xt[:, g2, u, :], in_=xw[:, 256 * g + u:256 * (g + 1):2],
                                            identity=ident_f[:])
                nc.scalar.copy(out=xg[:, 2 * gp:2 * gp + 2, :, :].bitcast(F32),
                               in_=xt[:].rearrange("p g u b -> p g b u"))

        def x_quant(bt):
            nc.vector.quantize_mx(out=xc[bt][:].bitcast(FP8X4), scales=xs[bt][:],
                                  in_=xgs[bt][:].rearrange("p g b t -> p (g b t)"))

        def norm_reduce():
            nc.vector.tensor_reduce(out=bnv[:], in_=small[:, 0:16 * JT].rearrange("p (s j) -> p j s", j=JT),
                                    axis=AX.X, op=ALU.add)

        def norm_spread(h):
            sp = psum.tile([P, HALF], F32, name="bank", tag="bank", bufs=7)
            for q in range(4):
                jt = 4 * h + q
                nc.tensor.transpose(out=sp[:, P * q:P * (q + 1)], in_=bnv[:, jt:jt + 1].to_broadcast([P, P]),
                                    identity=ident_f[:])
            nc.scalar.activation(out=bnb[:, HALF * h:HALF * (h + 1)], in_=sp[:], func=ACT.Copy, scale=-0.1)

        def y_term(bt):
            nc.gpsimd.tensor_tensor(out=o[:, bt, :], in0=y_sb[:, bt, :], in1=bnb[:], op=ALU.mult)

        def product(bt, h):
            hs = slice(HALF * h, HALF * (h + 1))
            acc = psum.tile([P, HALF], F32, name="bank", tag="bank", bufs=7)
            accs[(bt, h)] = acc
            for g in range(G):
                gs = slice(P * g, P * (g + 1))
                nc.tensor.matmul_mx(out=acc[:], lhsT=xc[bt][:, gs].bitcast(FP8X4), lhsT_scale=xs[bt][:, gs],
                                    rhs=bc[:, g, hs].bitcast(FP8X4), rhs_scale=bs[:, g, hs],
                                    start=(g == 0), stop=(g == G - 1))

        def add_y_term(bt, h):
            hs = slice(HALF * h, HALF * (h + 1))
            nc.vector.tensor_tensor(out=o[:, bt, hs], in0=accs[(bt, h)][:], in1=o[:, bt, hs], op=ALU.add)

        def w2_scalar(t):
            ws = w2[t][0]
            nc.scalar.activation(out=ws, in_=ws, func=ACT.Copy, scale=4096.0, accum_out=ss[:, t:t + 1])

        def w2_vector(t):
            wv = w2[t][1]
            nc.vector.tensor_scalar(out=wv, in0=wv, scalar1=4096.0, scalar2=cb[:, t:t + 1],
                                    op0=ALU.mult, op1=ALU.add, accum_out=sv[:, t:t + 1])

        def const_join(bi):
            t0, nt = BLOCKS[bi]
            nc.vector.tensor_tensor(out=cv[:, t0:t0 + nt], in0=sv[:, t0:t0 + nt], in1=ss[:, t0:t0 + nt], op=ALU.add)

        def const_spread(bi):
            t0, nt = BLOCKS[bi]
            sp = psum.tile([P, HALF], F32, name="bank", tag="bank", bufs=7)
            sps[bi] = sp
            for q in range(nt):
                nc.tensor.transpose(out=sp[:, P * q:P * (q + 1)], in_=cv[:, t0 + q:t0 + q + 1].to_broadcast([P, P]),
                                    identity=ident_f[:])

        def chunk_sum(bi, c):
            t0, nt = BLOCKS[bi]
            first = (t0 - NT) * P // RB
            if c == first:
                part = psum.tile([P, HALF], F32, name="bank", tag="bank", bufs=7)
                parts[bi] = part
            dst = parts[bi]
            col = RB * (c - first)
            if c == NCH - 1:
                last = psum.tile([P, HALF], F32, name="bank", tag="bank", bufs=7)
                parts["last"] = last
                dst = last
                col = 0
            for i in range(QW // P):
                nc.tensor.matmul(out=dst[:, col:col + RB], lhsT=wq[c][:, P * i:P * (i + 1)], rhs=sel32[:],
                                 start=(i == 0), stop=(i == QW // P - 1))

        def block_chunks(bi):
            t0, nt = BLOCKS[bi]
            return range((t0 - NT) * P // RB, (t0 + nt - NT) * P // RB)

        def part_out(bi):
            t0, nt = BLOCKS[bi]
            off = P * (t0 - NT)
            nc.scalar.activation(out=psb[:, off:off + P * nt], in_=parts[bi][:, 0:P * nt], func=ACT.Copy, scale=4096.0)

        def part_join(bi):
            t0, nt = BLOCKS[bi]
            sp = psum.tile([P, HALF], F32, name="bank", tag="bank", bufs=7)
            sps[bi] = sp
            for q in range(nt):
                off = P * (t0 + q - NT)
                nc.tensor.matmul(out=sp[:, P * q:P * (q + 1)], lhsT=cb[:, t0 + q:t0 + q + 1].to_broadcast([P, P]),
                                 rhs=ident_f[:], is_transpose=True, start=True, stop=False)
                nc.tensor.matmul(out=sp[:, P * q:P * (q + 1)], lhsT=ones_f[:], rhs=psb[:, off:off + P],
                                 start=False, stop=True)

        LB = len(BLOCKS) - 1
        LOFF = P * (JT - 1 - NT)
        LW = P - RB

        def last_out(step):
            if step == 0:
                nc.scalar.activation(out=psb[:, LOFF:LOFF + LW], in_=parts[LB][:, 0:LW], func=ACT.Copy, scale=4096.0)
            else:
                nc.scalar.activation(out=psb[:, LOFF + LW:LOFF + P], in_=parts["last"][:, 0:RB], func=ACT.Copy, scale=4096.0)

        def last_join(step):
            if step == 0:
                sp = psum.tile([P, HALF], F32, name="bank", tag="bank", bufs=7)
                sps[LB] = sp
                nc.tensor.matmul(out=sp[:, 0:P], lhsT=cb[:, JT - 1:JT].to_broadcast([P, P]), rhs=ident_f[:],
                                 is_transpose=True, start=True, stop=False)
            elif step == 1:
                nc.tensor.matmul(out=sps[LB][:, 0:LW], lhsT=ones_f[:], rhs=psb[:, LOFF:LOFF + LW], start=False, stop=False)
            else:
                nc.tensor.matmul(out=sps[LB][:, LW:P], lhsT=ones_f[:], rhs=psb[:, LOFF + LW:LOFF + P], start=False, stop=True)

        def block_cols(bi):
            t0, nt = BLOCKS[bi]
            return slice(P * t0, P * (t0 + nt)), nt * P

        def const_add(bi):
            js, w = block_cols(bi)
            nc.vector.tensor_tensor(out=o[:, :, js], in0=o[:, :, js],
                                    in1=sps[bi][:, 0:w].unsqueeze(1).to_broadcast([P, BT, w]), op=ALU.add)
            nc.sync.dma_start(out=out_0.rearrange("(p t) c -> p t c", t=BT)[:, :, js], in_=o[:, :, js])

        def add_v(bi):
            js, w = block_cols(bi)
            nc.vector.tensor_tensor(out=o[:, 0:2, js], in0=o[:, 0:2, js],
                                    in1=sps[bi][:, 0:w].unsqueeze(1).to_broadcast([P, 2, w]), op=ALU.add)

        def add_s(bi):
            js, w = block_cols(bi)
            nc.scalar.copy(out=csb[:, js], in_=sps[bi][:, 0:w])

        def add_g(bi):
            js, w = block_cols(bi)
            nc.gpsimd.tensor_tensor(out=o[:, 2:4, js], in0=o[:, 2:4, js],
                                    in1=csb[:, js].unsqueeze(1).to_broadcast([P, 2, w]), op=ALU.add)
            nc.sync.dma_start(out=out_0.rearrange("(p t) c -> p t c", t=BT)[:, :, js], in_=o[:, :, js])

        def row_max(bi, bt):
            js, w = block_cols(bi)
            nc.vector.tensor_reduce(out=pm[:, bt, bi:bi + 1], in_=o[:, bt, js], axis=AX.X, op=ALU.max,
                                    apply_absolute_value=True)

        with tc.manual_schedule():
            beta_copy(0, 0)
            beta_copy(0, 1)
            beta_abs(0, 0)
            beta_norm_part(0)
            beta_quant(0)
            beta_abs(1, 0)
            beta_norm_part(1)
            beta_copy(1, 0)
            beta_copy(1, 1)
            beta_abs(2, 0)
            beta_norm_part(2)
            beta_abs(3, 0)
            beta_norm_part(3)
            beta_quant(1)
            beta_copy(2, 0)
            beta_copy(2, 1)
            nc.tensor.matmul(out=small[:, 16 * JT:17 * JT], lhsT=brow[:], rhs=sel[:], start=True, stop=True)
            nc.vector.tensor_copy(out=cb[:], in_=small[:, 16 * JT:17 * JT])
            nc.vector.tensor_copy(out=sv[:], in_=small[:, 16 * JT:17 * JT])
            norm_reduce()
            beta_copy(3, 1)
            x_turn(0)
            norm_spread(0)
            norm_spread(1)
            beta_quant(2)
            beta_copy(3, 0)
            for bt in range(BT):
                y_term(bt)
            x_turn(1)
            x_turn(2)
            x_quant(0)
            beta_quant(3)
            x_turn(3)
            x_quant(1)
            product(0, 0)
            product(0, 1)
            x_quant(2)
            x_quant(3)
            w2_vector(1)
            w2_scalar(0)
            add_y_term(0, 0)
            add_y_term(0, 1)
            product(1, 0)
            product(1, 1)
            w2_scalar(2)
            add_y_term(1, 0)
            add_y_term(1, 1)
            w2_vector(2)
            product(2, 0)
            product(2, 1)
            add_y_term(2, 0)
            add_y_term(2, 1)
            product(3, 0)
            product(3, 1)
            add_y_term(3, 0)
            const_join(0)
            add_y_term(3, 1)
            for c in range(0, 4):
                chunk_sum(1, c)
            const_spread(0)
            for c in range(4, 8):
                chunk_sum(1, c)
            const_add(0)
            part_out(1)
            for c in range(8, 12):
                chunk_sum(2, c)
            part_join(1)
            part_out(2)
            row_max(0, 0)
            row_max(0, 1)
            row_max(0, 2)
            add_v(1)
            add_s(1)
            add_g(1)
            chunk_sum(3, 12)
            chunk_sum(3, 13)
            part_join(2)
            chunk_sum(3, 14)
            chunk_sum(3, 15)
            part_out(3)
            row_max(0, 3)
            row_max(1, 0)
            row_max(1, 1)
            add_v(2)
            add_s(2)
            add_g(2)
            chunk_sum(4, 16)
            chunk_sum(4, 17)
            part_join(3)
            chunk_sum(4, 18)
            last_out(0)
            last_join(0)
            chunk_sum(4, 19)
            last_out(1)
            last_join(1)
            last_join(2)
            row_max(2, 0)
            row_max(2, 1)
            row_max(1, 2)
            row_max(1, 3)
            add_v(3)
            add_s(3)
            add_g(3)
            row_max(3, 0)
            row_max(3, 1)
            row_max(2, 2)
            row_max(2, 3)
            const_add(4)
            row_max(3, 2)
            row_max(3, 3)
            row_max(4, 0)
            nc.vector.tensor_reduce(out=m1[:], in_=pm[:, :, 0:4], axis=AX.X, op=ALU.max)
            row_max(4, 1)
            nc.vector.reciprocal(out=r0[:], in_=m1[:])
            row_max(4, 2)
            nc.vector.tensor_scalar(out=r0[:], in0=r0[:], scalar1=448.0, scalar2=None, op0=ALU.mult)

            def last_reciprocal(b0, b1):
                nc.vector.reciprocal(out=r1[:, b0:b1], in_=pm[:, b0:b1, 4])

            def factor(b0, b1):
                nc.vector.scalar_tensor_tensor(out=rs[:, b0:b1], in0=r1[:, b0:b1], scalar=448.0, in1=r0[:, b0:b1],
                                               op0=ALU.mult, op1=ALU.min)

            def cast(bt, who):
                if who == "s":
                    nc.scalar.activation(out=o8[:, bt, :], in_=o[:, bt, :], func=ACT.Identity, scale=rs[:, bt:bt + 1],
                                         bias=zeros[:, 0:1], saturate=False)
                else:
                    nc.vector.tensor_scalar(out=o8[:, bt, :], in0=o[:, bt, :], scalar1=rs[:, bt:bt + 1], scalar2=None,
                                            op0=ALU.mult, saturate=False)
                nc.sync.dma_start(out=out_1.rearrange("(p t) c -> p t c", t=BT)[:, bt, :], in_=o8[:, bt, :].bitcast(U8))

            last_reciprocal(0, 2)
            row_max(4, 3)
            factor(0, 2)
            last_reciprocal(2, 4)
            cast(0, "s")
            cast(1, "v")
            factor(2, 4)
            cast(2, "v")
            cast(3, "v")
